import numpy as np
import ml_dtypes


def mxq(x, axis, fmt="e4m3"):
    dtype, down = {"e4m3": (ml_dtypes.float8_e4m3fn, 7), "e5m2": (ml_dtypes.float8_e5m2, 14)}[fmt]
    v = np.moveaxis(np.asarray(x, np.float32).astype(ml_dtypes.bfloat16).astype(np.float64), axis, -1)
    blocks = v.reshape(v.shape[:-1] + (-1, 32))
    amax = np.abs(blocks).max(-1, keepdims=True)
    byte = np.maximum(np.where(amax > 0, np.frexp(amax)[1] - 1 + 127, 0) - down, 1)
    scale = np.exp2(byte - 127.0)
    codes = (blocks / scale).astype(np.float32).astype(dtype).astype(np.float64)
    return np.moveaxis((codes * scale).reshape(v.shape), -1, axis)


WIDE = False


def mx_kscale(k):
    if not WIDE:
        return np.ones(k)
    levels = np.array([10, -10, 5, -5, 0])
    a = np.random.permutation(np.resize(levels, k // 512 * 4)).reshape(k // 512, 4)
    idx = np.arange(k)
    return np.exp2(a[idx // 512, idx % 128 // 32])


BF16 = ml_dtypes.bfloat16


def bf(x):
    return np.asarray(x, np.float32).astype(BF16)


def f64(x):
    return np.asarray(x).astype(np.float64)


B, G, Z1, Z2, H, PD = 256, 16, 256, 256, 512, 512
CIN = Z1 + Z2


def glin(x, W, b):
    y = mxq(x, 2, "e4m3").transpose(1, 0, 2) @ mxq(f64(W), 2, "e4m3").transpose(0, 2, 1)
    return y.transpose(1, 0, 2) + f64(b)


def setup_inputs():
    s = mx_kscale(CIN)
    return {"z1": bf((np.random.standard_normal((B, G, Z1)) * s[:Z1]).reshape(B, G * Z1)),
            "z2": bf((np.random.standard_normal((B, G, Z2)) * s[Z1:]).reshape(B, G * Z2)),
            "W1": bf(np.random.standard_normal((G, H, CIN)) / np.sqrt(CIN) / s),
            "b1": bf(np.random.standard_normal((G, H)) * 0.2),
            "W2": bf(np.random.standard_normal((G, H, H)) * 1.4 / np.sqrt(H)),
            "b2": bf(np.random.standard_normal((G, H)) * 0.2)}


def reference(z1, z2, W1, b1, W2, b2):
    z = np.concatenate([f64(z1).reshape(B, G, Z1), f64(z2).reshape(B, G, Z2)], axis=2)
    h1 = np.maximum(glin(z, W1, b1), 0.0)
    return np.maximum(glin(h1, W2, b2), 0.0) + h1

@@ -1,0 +1,194 @@
+from contextlib import ExitStack
+
+import concourse.mybir as mybir
+from concourse.masks import make_identity
+
+F32 = mybir.dt.float32
+BF16 = mybir.dt.bfloat16
+U32 = mybir.dt.uint32
+U8 = mybir.dt.uint8
+FP8X4 = mybir.dt.float8_e4m3fn_x4
+ALU = mybir.AluOpType
+ACT = mybir.ActivationFunctionType
+
+P = 128
+B, G, H = 256, 16, 512
+ZG = 4
+FLOPS = 2 * B * H * H * G * 2
+
+
+def tile_linearwdecoder_pa_kernel(tc, z1, z2, W1, b1, W2, b2, out):
+    nc = tc.nc
+    with ExitStack() as ctx:
+        const = ctx.enter_context(tc.tile_pool(name="const", bufs=1))
+        zpool = ctx.enter_context(tc.tile_pool(name="zpool", bufs=4))
+        wpool = ctx.enter_context(tc.tile_pool(name="wpool", bufs=5))
+        gpool = ctx.enter_context(tc.tile_pool(name="gpool", bufs=2))
+        cpool = ctx.enter_context(tc.tile_pool(name="cpool", bufs=3))
+        hpool = ctx.enter_context(tc.tile_pool(name="hpool", bufs=3))
+        opool = ctx.enter_context(tc.tile_pool(name="opool", bufs=3))
+        tps = ctx.enter_context(tc.psum_pool(name="tps", bufs=4))
+        mps = ctx.enter_context(tc.psum_pool(name="mps", bufs=4))
+
+        ident = const.tile([P, P], F32)
+        make_identity(nc, ident[:])
+
+        braw = const.tile([P, 256], BF16)
+        nc.vector.memset(braw[:], 0.0)
+        nc.sync.dma_start(out=braw[0:32, :], in_=b1.rearrange("g (u c) -> (g u) c", u=2))
+        bsplit = const.tile([P, 2, P], F32)
+        nc.vector.tensor_copy(out=bsplit[:], in_=braw[:].rearrange("r (p e) -> r e p", e=2))
+        b1T = const.tile([P, 2, 32], F32)
+        bt = tps.tile([P, 512], F32, tag="tp")
+        for e in range(2):
+            nc.tensor.transpose(bt[:, e * P:(e + 1) * P], bsplit[:, e, :], ident[:])
+        nc.vector.tensor_copy(
+            out=b1T[:], in_=bt[:, 0:256].rearrange("p (e r) -> p e r", e=2)[:, :, 0:32])
+
+        b2bc = const.tile([P, G * H], BF16)
+
+        zraws = {}
+        wraws = {}
+        st = {}
+
+        def load_z(q):
+            zraw = zpool.tile([P, 4096], BF16, tag="zraw")
+            for u, src in enumerate((z1, z2)):
+                nc.sync.dma_start(
+                    out=zraw[:, u * 2048:(u + 1) * 2048].rearrange("p (c k) -> p c k", c=2),
+                    in_=src[:, q * 1024:(q + 1) * 1024].rearrange("(c p) k -> p c k", p=P))
+            zraws[q] = zraw
+
+        def load_w(g):
+            wraw = wpool.tile([P, 4096], BF16, tag="wraw")
+            for i, src in enumerate((W1, W2)):
+                nc.sync.dma_start(
+                    out=wraw[:, i * 2048:(i + 1) * 2048].rearrange("p (u c) -> p u c", u=2),
+                    in_=src[g].rearrange("(u j e) k -> j u (e k)", u=2, e=2))
+            wraws[g] = wraw
+
+        def evac(dst_words, bank):
+            nc.scalar.copy(out=dst_words.rearrange("p (c u) -> p c u", u=2),
+                           in_=bank[:].rearrange("p (u c) -> p c u", u=2))
+
+        def stage_a(g):
+            zw = zraws[g // ZG][:].bitcast(F32)
+            gl = g % ZG
+            ww = wraws[g][:].bitcast(F32)
+            grz = gpool.tile([P, 1024], BF16, tag="grz", align_bytes=64)
+            grw = gpool.tile([P, 4096], BF16, tag="grw", align_bytes=64)
+            zt = tps.tile([P, 512], F32, tag="tp")
+            for u in range(2):
+                for c in range(2):
+                    o = (u * 2 + c) * 512 + gl * P
+                    nc.tensor.transpose(zt[:, u * 256 + c * P: u * 256 + (c + 1) * P],
+                                        zw[:, o:o + P], ident[:])
+            evac(grz[:].bitcast(F32), zt)
+            for v in range(4):
+                wt = tps.tile([P, 512], F32, tag="tp")
+                for half in range(2):
+                    if v < 2:
+                        chunk = 2 * v + half
+                    else:
+                        chunk = 4 + 2 * half + (v - 2)
+                    for uw in range(2):
+                        o = chunk * 256 + uw * P
+                        nc.tensor.transpose(wt[:, uw * 256 + half * P: uw * 256 + (half + 1) * P],
+                                            ww[:, o:o + P], ident[:])
+                evac(grw[:].bitcast(F32)[:, v * 512:(v + 1) * 512], wt)
+            cz = cpool.tile([P, 256], U32, tag="cz", align_bytes=64)
+            sz = cpool.tile([P, 256], U8, tag="sz", align_bytes=64)
+            cw = cpool.tile([P, 1024], U32, tag="cw", align_bytes=64)
+            sw = cpool.tile([P, 1024], U8, tag="sw", align_bytes=64)
+            nc.vector.quantize_mx(out=cz[:].bitcast(FP8X4), scales=sz[:], in_=grz[:])
+            nc.vector.quantize_mx(out=cw[:].bitcast(FP8X4), scales=sw[:], in_=grw[:])
+            st[g] = {"cz": cz, "sz": sz, "cw": cw, "sw": sw}
+
+        def stage_b(g):
+            s = st[g]
+            h1T = hpool.tile([P, 4, 256], F32, tag="h1T")
+            for v in range(2):
+                y1 = mps.tile([P, 512], F32, tag="mm")
+                for half in range(2):
+                    t = 2 * v + half
+                    nc.tensor.matmul_mx(
+                        out=y1[:, half * 256:(half + 1) * 256],
+                        lhsT=s["cw"][:, t * P:(t + 1) * P].bitcast(FP8X4),
+                        lhsT_scale=s["sw"][:, t * P:(t + 1) * P],
+                        rhs=s["cz"][:].bitcast(FP8X4), rhs_scale=s["sz"][:],
+                        start=True, stop=True)
+                for half in range(2):
+                    t = 2 * v + half
+                    nc.scalar.activation(
+                        out=h1T[:, t, :], in_=y1[:, half * 256:(half + 1) * 256], func=ACT.Relu,
+                        bias=b1T[:, half, 2 * g + v:2 * g + v + 1], scale=1.0)
+            grh = gpool.tile([P, 1024], BF16, tag="grh", align_bytes=64)
+            nc.gpsimd.tensor_scalar(
+                out=grh[:].rearrange("p (b t) -> p b t", t=4),
+                in0=h1T[:].rearrange("p t b -> p b t"),
+                scalar1=1.0, scalar2=0.0, op0=ALU.mult, op1=ALU.add)
+            ch = cpool.tile([P, 256], U32, tag="ch", align_bytes=64)
+            sh = cpool.tile([P, 256], U8, tag="sh", align_bytes=64)
+            nc.vector.quantize_mx(out=ch[:].bitcast(FP8X4), scales=sh[:], in_=grh[:])
+            s["h1T"] = h1T
+            s["ch"] = ch
+            s["sh"] = sh
+
+        def stage_th(g):
+            s = st[g]
+            h1T = s["h1T"]
+            hns = []
+            for c in range(2):
+                hn = tps.tile([P, 512], F32, tag="tp")
+                for t in range(4):
+                    pos = 2 * (t % 2) + t // 2
+                    nc.tensor.transpose(hn[:, pos * P:(pos + 1) * P],
+                                        h1T[:, t, c * P:(c + 1) * P], ident[:])
+                hns.append(hn)
+            s["hns"] = hns
+
+        def stage_c(g):
+            s = st[g]
+            hns = s["hns"]
+            osb = opool.tile([P, 2, H], F32, tag="osb")
+            for c in range(2):
+                y2 = mps.tile([P, 512], F32, tag="mm")
+                nc.tensor.matmul_mx(
+                    out=y2[:],
+                    lhsT=s["ch"][:, c * P:(c + 1) * P].bitcast(FP8X4),
+                    lhsT_scale=s["sh"][:, c * P:(c + 1) * P],
+                    rhs=s["cw"][:, 512:1024].bitcast(FP8X4), rhs_scale=s["sw"][:, 512:1024],
+                    start=True, stop=True)
+                tmp = opool.tile([P, H], F32, tag="tmp")
+                nc.vector.tensor_tensor(
+                    out=tmp[:].rearrange("p (j e) -> p j e", e=2),
+                    in0=y2[:].rearrange("p (e j) -> p j e", e=2),
+                    in1=b2bc[:, g * H:(g + 1) * H].rearrange("p (j e) -> p j e", e=2),
+                    op=ALU.add)
+                nc.vector.scalar_tensor_tensor(
+                    out=osb[:, c, :].rearrange("p (j e) -> p j e", e=2),
+                    in0=tmp[:].rearrange("p (j e) -> p j e", e=2),
+                    scalar=0.0,
+                    in1=hns[c][:].rearrange("p (e j) -> p j e", e=2),
+                    op0=ALU.max, op1=ALU.add)
+            nc.sync.dma_start(out=out[:, g, :].rearrange("(c p) m -> p c m", p=P), in_=osb[:])
+
+        load_z(0)
+        load_w(0)
+        load_w(1)
+        nc.sync.dma_start(out=b2bc[:], in_=b2.rearrange("g m -> (g m)").partition_broadcast(P))
+        load_w(2)
+        for i in range(G + 2):
+            nxt = i + 3
+            if nxt < G:
+                if nxt % ZG == 0:
+                    load_z(nxt // ZG)
+                load_w(nxt)
+            if i < G:
+                stage_a(i)
+            if i >= 2:
+                stage_th(i - 2)
+            if 1 <= i <= G:
+                stage_b(i - 1)
+            if i >= 2:
+                stage_c(i - 2)

@@ -14,6 +14,7 @@ ACT = mybir.ActivationFunctionType
 P = 128
 B, G, H = 256, 16, 512
 ZG = 4
+PRE = 4
 FLOPS = 2 * B * H * H * G * 2
 
 
@@ -22,34 +23,27 @@ def tile_linearwdecoder_pa_kernel(tc, z1, z2, W1, b1, W2, b2, out):
     with ExitStack() as ctx:
         const = ctx.enter_context(tc.tile_pool(name="const", bufs=1))
         zpool = ctx.enter_context(tc.tile_pool(name="zpool", bufs=4))
-        wpool = ctx.enter_context(tc.tile_pool(name="wpool", bufs=5))
+        wpool = ctx.enter_context(tc.tile_pool(name="wpool", bufs=6))
         gpool = ctx.enter_context(tc.tile_pool(name="gpool", bufs=2))
         cpool = ctx.enter_context(tc.tile_pool(name="cpool", bufs=3))
         hpool = ctx.enter_context(tc.tile_pool(name="hpool", bufs=3))
         opool = ctx.enter_context(tc.tile_pool(name="opool", bufs=3))
-        tps = ctx.enter_context(tc.psum_pool(name="tps", bufs=4))
-        mps = ctx.enter_context(tc.psum_pool(name="mps", bufs=4))
+        tps = ctx.enter_context(tc.psum_pool(name="tps", bufs=3))
+        hps = ctx.enter_context(tc.psum_pool(name="hps", bufs=2))
+        mps = ctx.enter_context(tc.psum_pool(name="mps", bufs=3))
+        ctx.enter_context(tc.manual_schedule())
 
-        ident = const.tile([P, P], F32)
-        make_identity(nc, ident[:])
-
-        braw = const.tile([P, 256], BF16)
-        nc.vector.memset(braw[:], 0.0)
-        nc.sync.dma_start(out=braw[0:32, :], in_=b1.rearrange("g (u c) -> (g u) c", u=2))
-        bsplit = const.tile([P, 2, P], F32)
-        nc.vector.tensor_copy(out=bsplit[:], in_=braw[:].rearrange("r (p e) -> r e p", e=2))
-        b1T = const.tile([P, 2, 32], F32)
-        bt = tps.tile([P, 512], F32, tag="tp")
-        for e in range(2):
-            nc.tensor.transpose(bt[:, e * P:(e + 1) * P], bsplit[:, e, :], ident[:])
-        nc.vector.tensor_copy(
-            out=b1T[:], in_=bt[:, 0:256].rearrange("p (e r) -> p e r", e=2)[:, :, 0:32])
+        zraws = {}
+        st = {}
+        for g in range(G):
+            st[g] = {}
 
         b2bc = const.tile([P, G * H], BF16)
 
-        zraws = {}
-        wraws = {}
-        st = {}
+        def load_b2(q):
+            nc.sync.dma_start(
+                out=b2bc[:, q * ZG * H:(q + 1) * ZG * H],
+                in_=b2[q * ZG:(q + 1) * ZG, :].rearrange("g m -> (g m)").partition_broadcast(P))
 
         def load_z(q):
             zraw = zpool.tile([P, 4096], BF16, tag="zraw")
@@ -65,130 +59,194 @@ def tile_linearwdecoder_pa_kernel(tc, z1, z2, W1, b1, W2, b2, out):
                 nc.sync.dma_start(
                     out=wraw[:, i * 2048:(i + 1) * 2048].rearrange("p (u c) -> p u c", u=2),
                     in_=src[g].rearrange("(u j e) k -> j u (e k)", u=2, e=2))
-            wraws[g] = wraw
+            st[g]["wraw"] = wraw
 
-        def evac(dst_words, bank):
-            nc.scalar.copy(out=dst_words.rearrange("p (c u) -> p c u", u=2),
-                           in_=bank[:].rearrange("p (u c) -> p c u", u=2))
-
-        def stage_a(g):
-            zw = zraws[g // ZG][:].bitcast(F32)
-            gl = g % ZG
-            ww = wraws[g][:].bitcast(F32)
-            grz = gpool.tile([P, 1024], BF16, tag="grz", align_bytes=64)
-            grw = gpool.tile([P, 4096], BF16, tag="grw", align_bytes=64)
-            zt = tps.tile([P, 512], F32, tag="tp")
-            for u in range(2):
-                for c in range(2):
-                    o = (u * 2 + c) * 512 + gl * P
-                    nc.tensor.transpose(zt[:, u * 256 + c * P: u * 256 + (c + 1) * P],
-                                        zw[:, o:o + P], ident[:])
-            evac(grz[:].bitcast(F32), zt)
-            for v in range(4):
-                wt = tps.tile([P, 512], F32, tag="tp")
-                for half in range(2):
-                    if v < 2:
-                        chunk = 2 * v + half
-                    else:
-                        chunk = 4 + 2 * half + (v - 2)
-                    for uw in range(2):
-                        o = chunk * 256 + uw * P
-                        nc.tensor.transpose(wt[:, uw * 256 + half * P: uw * 256 + (half + 1) * P],
-                                            ww[:, o:o + P], ident[:])
-                evac(grw[:].bitcast(F32)[:, v * 512:(v + 1) * 512], wt)
-            cz = cpool.tile([P, 256], U32, tag="cz", align_bytes=64)
-            sz = cpool.tile([P, 256], U8, tag="sz", align_bytes=64)
-            cw = cpool.tile([P, 1024], U32, tag="cw", align_bytes=64)
-            sw = cpool.tile([P, 1024], U8, tag="sw", align_bytes=64)
-            nc.vector.quantize_mx(out=cz[:].bitcast(FP8X4), scales=sz[:], in_=grz[:])
-            nc.vector.quantize_mx(out=cw[:].bitcast(FP8X4), scales=sw[:], in_=grw[:])
-            st[g] = {"cz": cz, "sz": sz, "cw": cw, "sw": sw}
-
-        def stage_b(g):
-            s = st[g]
-            h1T = hpool.tile([P, 4, 256], F32, tag="h1T")
-            for v in range(2):
-                y1 = mps.tile([P, 512], F32, tag="mm")
-                for half in range(2):
-                    t = 2 * v + half
-                    nc.tensor.matmul_mx(
-                        out=y1[:, half * 256:(half + 1) * 256],
-                        lhsT=s["cw"][:, t * P:(t + 1) * P].bitcast(FP8X4),
-                        lhsT_scale=s["sw"][:, t * P:(t + 1) * P],
-                        rhs=s["cz"][:].bitcast(FP8X4), rhs_scale=s["sz"][:],
-                        start=True, stop=True)
-                for half in range(2):
-                    t = 2 * v + half
-                    nc.scalar.activation(
-                        out=h1T[:, t, :], in_=y1[:, half * 256:(half + 1) * 256], func=ACT.Relu,
-                        bias=b1T[:, half, 2 * g + v:2 * g + v + 1], scale=1.0)
-            grh = gpool.tile([P, 1024], BF16, tag="grh", align_bytes=64)
-            nc.gpsimd.tensor_scalar(
-                out=grh[:].rearrange("p (b t) -> p b t", t=4),
-                in0=h1T[:].rearrange("p t b -> p b t"),
-                scalar1=1.0, scalar2=0.0, op0=ALU.mult, op1=ALU.add)
-            ch = cpool.tile([P, 256], U32, tag="ch", align_bytes=64)
-            sh = cpool.tile([P, 256], U8, tag="sh", align_bytes=64)
-            nc.vector.quantize_mx(out=ch[:].bitcast(FP8X4), scales=sh[:], in_=grh[:])
-            s["h1T"] = h1T
-            s["ch"] = ch
-            s["sh"] = sh
-
-        def stage_th(g):
-            s = st[g]
-            h1T = s["h1T"]
-            hns = []
-            for c in range(2):
-                hn = tps.tile([P, 512], F32, tag="tp")
-                for t in range(4):
-                    pos = 2 * (t % 2) + t // 2
-                    nc.tensor.transpose(hn[:, pos * P:(pos + 1) * P],
-                                        h1T[:, t, c * P:(c + 1) * P], ident[:])
-                hns.append(hn)
-            s["hns"] = hns
-
-        def stage_c(g):
-            s = st[g]
-            hns = s["hns"]
-            osb = opool.tile([P, 2, H], F32, tag="osb")
-            for c in range(2):
-                y2 = mps.tile([P, 512], F32, tag="mm")
-                nc.tensor.matmul_mx(
-                    out=y2[:],
-                    lhsT=s["ch"][:, c * P:(c + 1) * P].bitcast(FP8X4),
-                    lhsT_scale=s["sh"][:, c * P:(c + 1) * P],
-                    rhs=s["cw"][:, 512:1024].bitcast(FP8X4), rhs_scale=s["sw"][:, 512:1024],
-                    start=True, stop=True)
-                tmp = opool.tile([P, H], F32, tag="tmp")
-                nc.vector.tensor_tensor(
-                    out=tmp[:].rearrange("p (j e) -> p j e", e=2),
-                    in0=y2[:].rearrange("p (e j) -> p j e", e=2),
-                    in1=b2bc[:, g * H:(g + 1) * H].rearrange("p (j e) -> p j e", e=2),
-                    op=ALU.add)
-                nc.vector.scalar_tensor_tensor(
-                    out=osb[:, c, :].rearrange("p (j e) -> p j e", e=2),
-                    in0=tmp[:].rearrange("p (j e) -> p j e", e=2),
-                    scalar=0.0,
-                    in1=hns[c][:].rearrange("p (e j) -> p j e", e=2),
-                    op0=ALU.max, op1=ALU.add)
-            nc.sync.dma_start(out=out[:, g, :].rearrange("(c p) m -> p c m", p=P), in_=osb[:])
-
+        braw = const.tile([P, 256], BF16)
+        nc.vector.memset(braw[:], 0.0)
+        nc.sync.dma_start(out=braw[0:32, :], in_=b1.rearrange("g (u c) -> (g u) c", u=2))
         load_z(0)
         load_w(0)
         load_w(1)
-        nc.sync.dma_start(out=b2bc[:], in_=b2.rearrange("g m -> (g m)").partition_broadcast(P))
         load_w(2)
-        for i in range(G + 2):
-            nxt = i + 3
+        load_b2(0)
+        load_w(3)
+
+        ident = const.tile([P, P], F32)
+        make_identity(nc, ident[:])
+        bsplit = const.tile([P, 2, P], F32)
+        nc.vector.tensor_copy(out=bsplit[:], in_=braw[:].rearrange("r (p e) -> r e p", e=2))
+        b1T = const.tile([P, 2, 32], F32)
+        bt = tps.tile([P, 512], F32, tag="tp")
+        for e in range(2):
+            nc.tensor.transpose(bt[:, e * P:(e + 1) * P], bsplit[:, e, :], ident[:])
+        nc.vector.tensor_copy(
+            out=b1T[:], in_=bt[:, 0:256].rearrange("p (e r) -> p e r", e=2)[:, :, 0:32])
+
+        def ta(g, k):
+            s = st[g]
+            bank = tps.tile([P, 512], F32, tag="tp")
+            if k == 0:
+                words = zraws[g // ZG][:].bitcast(F32)
+                offs = [(u * 2 + c) * 512 + (g % ZG) * P for u in range(2) for c in range(2)]
+            else:
+                words = s["wraw"][:].bitcast(F32)
+                v = k - 1
+                chunks = [2 * v, 2 * v + 1] if v < 2 else [4 + (v - 2), 6 + (v - 2)]
+                offs = [chunks[half] * 256 + uw * P for uw in range(2) for half in range(2)]
+            for n, o in enumerate(offs):
+                nc.tensor.transpose(bank[:, n * P:(n + 1) * P], words[:, o:o + P], ident[:])
+            s["bank%d" % k] = bank
+
+        def ev(g, k):
+            s = st[g]
+            if k == 0:
+                grz = gpool.tile([P, 1024], BF16, tag="grz", align_bytes=64)
+                s["grz"] = grz
+                dst = grz[:].bitcast(F32)
+            else:
+                if k == 1:
+                    grw = gpool.tile([P, 4096], BF16, tag="grw", align_bytes=64)
+                    s["grw"] = grw
+                dst = s["grw"][:].bitcast(F32)[:, (k - 1) * 512:k * 512]
+            nc.scalar.copy(out=dst.rearrange("p (c u) -> p c u", u=2),
+                           in_=s["bank%d" % k][:].rearrange("p (u c) -> p c u", u=2))
+
+        def qz(g):
+            s = st[g]
+            cz = cpool.tile([P, 256], U32, tag="cz", align_bytes=64)
+            sz = cpool.tile([P, 256], U8, tag="sz", align_bytes=64)
+            nc.vector.quantize_mx(out=cz[:].bitcast(FP8X4), scales=sz[:], in_=s["grz"][:])
+            s["cz"] = cz
+            s["sz"] = sz
+
+        def qw(g):
+            s = st[g]
+            cw = cpool.tile([P, 1024], U32, tag="cw", align_bytes=64)
+            sw = cpool.tile([P, 1024], U8, tag="sw", align_bytes=64)
+            nc.vector.quantize_mx(out=cw[:].bitcast(FP8X4), scales=sw[:], in_=s["grw"][:])
+            s["cw"] = cw
+            s["sw"] = sw
+
+        def l1(g, v):
+            s = st[g]
+            y1 = mps.tile([P, 512], F32, tag="mm")
+            for half in range(2):
+                t = 2 * v + half
+                nc.tensor.matmul_mx(
+                    out=y1[:, half * 256:(half + 1) * 256],
+                    lhsT=s["cw"][:, t * P:(t + 1) * P].bitcast(FP8X4),
+                    lhsT_scale=s["sw"][:, t * P:(t + 1) * P],
+                    rhs=s["cz"][:].bitcast(FP8X4), rhs_scale=s["sz"][:],
+                    start=True, stop=True)
+            s["y1_%d" % v] = y1
+
+        def p1(g, v):
+            s = st[g]
+            if v == 0:
+                h1T = hpool.tile([P, 4, 256], F32, tag="h1T")
+                s["h1T"] = h1T
+            for half in range(2):
+                nc.scalar.activation(
+                    out=s["h1T"][:, 2 * v + half, :],
+                    in_=s["y1_%d" % v][:, half * 256:(half + 1) * 256], func=ACT.Relu,
+                    bias=b1T[:, half, 2 * g + v:2 * g + v + 1], scale=1.0)
+
+        def p2(g):
+            s = st[g]
+            grh = gpool.tile([P, 1024], BF16, tag="grh", align_bytes=64)
+            nc.gpsimd.tensor_scalar(
+                out=grh[:].rearrange("p (b t) -> p b t", t=4),
+                in0=s["h1T"][:].rearrange("p t b -> p b t"),
+                scalar1=1.0, scalar2=0.0, op0=ALU.mult, op1=ALU.add)
+            s["grh"] = grh
+
+        def qh(g):
+            s = st[g]
+            ch = cpool.tile([P, 256], U32, tag="ch", align_bytes=64)
+            sh = cpool.tile([P, 256], U8, tag="sh", align_bytes=64)
+            nc.vector.quantize_mx(out=ch[:].bitcast(FP8X4), scales=sh[:], in_=s["grh"][:])
+            s["ch"] = ch
+            s["sh"] = sh
+
+        def th(g, c):
+            s = st[g]
+            hn = hps.tile([P, 512], F32, tag="hn")
+            for t in range(4):
+                pos = 2 * (t % 2) + t // 2
+                nc.tensor.transpose(hn[:, pos * P:(pos + 1) * P],
+                                    s["h1T"][:, t, c * P:(c + 1) * P], ident[:])
+            s["hn%d" % c] = hn
+
+        def l2(g, c):
+            s = st[g]
+            y2 = mps.tile([P, 512], F32, tag="mm")
+            nc.tensor.matmul_mx(
+                out=y2[:],
+                lhsT=s["ch"][:, c * P:(c + 1) * P].bitcast(FP8X4),
+                lhsT_scale=s["sh"][:, c * P:(c + 1) * P],
+                rhs=s["cw"][:, 512:1024].bitcast(FP8X4), rhs_scale=s["sw"][:, 512:1024],
+                start=True, stop=True)
+            s["y2_%d" % c] = y2
+
+        def pa(g, c):
+            s = st[g]
+            tmp = opool.tile([P, H], F32, tag="tmp")
+            nc.vector.tensor_tensor(
+                out=tmp[:].rearrange("p (j e) -> p j e", e=2),
+                in0=s["y2_%d" % c][:].rearrange("p (e j) -> p j e", e=2),
+                in1=b2bc[:, g * H:(g + 1) * H].rearrange("p (j e) -> p j e", e=2),
+                op=ALU.add)
+            s["tmp"] = tmp
+
+        def pb(g, c):
+            s = st[g]
+            if c == 0:
+                osb = opool.tile([P, 2, H], F32, tag="osb")
+                s["osb"] = osb
+            nc.vector.scalar_tensor_tensor(
+                out=s["osb"][:, c, :].rearrange("p (j e) -> p j e", e=2),
+                in0=s["tmp"][:].rearrange("p (j e) -> p j e", e=2),
+                scalar=0.0,
+                in1=s["hn%d" % c][:].rearrange("p (e j) -> p j e", e=2),
+                op0=ALU.max, op1=ALU.add)
+
+        def store(g):
+            nc.sync.dma_start(out=out[:, g, :].rearrange("(c p) m -> p c m", p=P),
+                              in_=st[g]["osb"][:])
+
+        def live(g):
+            return 0 <= g < G
+
+        for i in range(G + 3):
+            nxt = i + PRE
             if nxt < G:
                 if nxt % ZG == 0:
                     load_z(nxt // ZG)
                 load_w(nxt)
-            if i < G:
-                stage_a(i)
-            if i >= 2:
-                stage_th(i - 2)
-            if 1 <= i <= G:
-                stage_b(i - 1)
-            if i >= 2:
-                stage_c(i - 2)
+                if nxt % ZG == 1:
+                    load_b2(nxt // ZG)
+            if live(i - 3):
+                for c in range(2):
+                    pa(i - 3, c)
+                    pb(i - 3, c)
+                store(i - 3)
+            if live(i):
+                for k in range(5):
+                    ta(i, k)
+                    ev(i, k)
+            if live(i - 2):
+                th(i - 2, 0)
+                th(i - 2, 1)
+            if live(i - 1):
+                l1(i - 1, 0)
+                l1(i - 1, 1)
+                p1(i - 1, 0)
+                p1(i - 1, 1)
+            if live(i - 2):
+                p2(i - 2)
+                qh(i - 2)
+                l2(i - 2, 0)
+                l2(i - 2, 1)
+            if live(i):
+                qz(i)
+                qw(i)

@@ -231,15 +231,20 @@ def tile_linearwdecoder_pa_kernel(tc, z1, z2, W1, b1, W2, b2, out):
                     pb(i - 3, c)
                 store(i - 3)
             if live(i):
-                for k in range(5):
+                for k in range(3):
+                    ta(i, k)
+                    ev(i, k)
+            if live(i - 1):
+                l1(i - 1, 0)
+                l1(i - 1, 1)
+            if live(i):
+                for k in range(3, 5):
                     ta(i, k)
                     ev(i, k)
             if live(i - 2):
                 th(i - 2, 0)
                 th(i - 2, 1)
             if live(i - 1):
-                l1(i - 1, 0)
-                l1(i - 1, 1)
                 p1(i - 1, 0)
                 p1(i - 1, 1)
             if live(i - 2):

@@ -28,9 +28,7 @@ def tile_linearwdecoder_pa_kernel(tc, z1, z2, W1, b1, W2, b2, out):
         cpool = ctx.enter_context(tc.tile_pool(name="cpool", bufs=3))
         hpool = ctx.enter_context(tc.tile_pool(name="hpool", bufs=3))
         opool = ctx.enter_context(tc.tile_pool(name="opool", bufs=3))
-        tps = ctx.enter_context(tc.psum_pool(name="tps", bufs=3))
-        hps = ctx.enter_context(tc.psum_pool(name="hps", bufs=2))
-        mps = ctx.enter_context(tc.psum_pool(name="mps", bufs=3))
+        psum = ctx.enter_context(tc.psum_pool(name="psum", bufs=8))
         ctx.enter_context(tc.manual_schedule())
 
         zraws = {}
@@ -76,7 +74,7 @@ def tile_linearwdecoder_pa_kernel(tc, z1, z2, W1, b1, W2, b2, out):
         bsplit = const.tile([P, 2, P], F32)
         nc.vector.tensor_copy(out=bsplit[:], in_=braw[:].rearrange("r (p e) -> r e p", e=2))
         b1T = const.tile([P, 2, 32], F32)
-        bt = tps.tile([P, 512], F32, tag="tp")
+        bt = psum.tile([P, 512], F32, tag="ps")
         for e in range(2):
             nc.tensor.transpose(bt[:, e * P:(e + 1) * P], bsplit[:, e, :], ident[:])
         nc.vector.tensor_copy(
@@ -84,7 +82,7 @@ def tile_linearwdecoder_pa_kernel(tc, z1, z2, W1, b1, W2, b2, out):
 
         def ta(g, k):
             s = st[g]
-            bank = tps.tile([P, 512], F32, tag="tp")
+            bank = psum.tile([P, 512], F32, tag="ps")
             if k == 0:
                 words = zraws[g // ZG][:].bitcast(F32)
                 offs = [(u * 2 + c) * 512 + (g % ZG) * P for u in range(2) for c in range(2)]
@@ -119,17 +117,20 @@ def tile_linearwdecoder_pa_kernel(tc, z1, z2, W1, b1, W2, b2, out):
             s["cz"] = cz
             s["sz"] = sz
 
-        def qw(g):
+        def qw(g, i):
             s = st[g]
-            cw = cpool.tile([P, 1024], U32, tag="cw", align_bytes=64)
-            sw = cpool.tile([P, 1024], U8, tag="sw", align_bytes=64)
-            nc.vector.quantize_mx(out=cw[:].bitcast(FP8X4), scales=sw[:], in_=s["grw"][:])
-            s["cw"] = cw
-            s["sw"] = sw
+            if i == 0:
+                cw = cpool.tile([P, 1024], U32, tag="cw", align_bytes=64)
+                sw = cpool.tile([P, 1024], U8, tag="sw", align_bytes=64)
+                s["cw"] = cw
+                s["sw"] = sw
+            nc.vector.quantize_mx(out=s["cw"][:, i * 512:(i + 1) * 512].bitcast(FP8X4),
+                                  scales=s["sw"][:, i * 512:(i + 1) * 512],
+                                  in_=s["grw"][:, i * 2048:(i + 1) * 2048])
 
         def l1(g, v):
             s = st[g]
-            y1 = mps.tile([P, 512], F32, tag="mm")
+            y1 = psum.tile([P, 512], F32, tag="ps")
             for half in range(2):
                 t = 2 * v + half
                 nc.tensor.matmul_mx(
@@ -170,7 +171,7 @@ def tile_linearwdecoder_pa_kernel(tc, z1, z2, W1, b1, W2, b2, out):
 
         def th(g, c):
             s = st[g]
-            hn = hps.tile([P, 512], F32, tag="hn")
+            hn = psum.tile([P, 512], F32, tag="ps")
             for t in range(4):
                 pos = 2 * (t % 2) + t // 2
                 nc.tensor.transpose(hn[:, pos * P:(pos + 1) * P],
@@ -179,7 +180,7 @@ def tile_linearwdecoder_pa_kernel(tc, z1, z2, W1, b1, W2, b2, out):
 
         def l2(g, c):
             s = st[g]
-            y2 = mps.tile([P, 512], F32, tag="mm")
+            y2 = psum.tile([P, 512], F32, tag="ps")
             nc.tensor.matmul_mx(
                 out=y2[:],
                 lhsT=s["ch"][:, c * P:(c + 1) * P].bitcast(FP8X4),
@@ -196,7 +197,7 @@ def tile_linearwdecoder_pa_kernel(tc, z1, z2, W1, b1, W2, b2, out):
                 in0=s["y2_%d" % c][:].rearrange("p (e j) -> p j e", e=2),
                 in1=b2bc[:, g * H:(g + 1) * H].rearrange("p (j e) -> p j e", e=2),
                 op=ALU.add)
-            s["tmp"] = tmp
+            s["tmp%d" % c] = tmp
 
         def pb(g, c):
             s = st[g]
@@ -205,7 +206,7 @@ def tile_linearwdecoder_pa_kernel(tc, z1, z2, W1, b1, W2, b2, out):
                 s["osb"] = osb
             nc.vector.scalar_tensor_tensor(
                 out=s["osb"][:, c, :].rearrange("p (j e) -> p j e", e=2),
-                in0=s["tmp"][:].rearrange("p (j e) -> p j e", e=2),
+                in0=s["tmp%d" % c][:].rearrange("p (j e) -> p j e", e=2),
                 scalar=0.0,
                 in1=s["hn%d" % c][:].rearrange("p (e j) -> p j e", e=2),
                 op0=ALU.max, op1=ALU.add)
@@ -217,41 +218,53 @@ def tile_linearwdecoder_pa_kernel(tc, z1, z2, W1, b1, W2, b2, out):
         def live(g):
             return 0 <= g < G
 
-        for i in range(G + 3):
-            nxt = i + PRE
+        for k in range(3):
+            ta(0, k)
+        for c in range(G + 3):
+            nxt = c + PRE
             if nxt < G:
                 if nxt % ZG == 0:
                     load_z(nxt // ZG)
                 load_w(nxt)
                 if nxt % ZG == 1:
                     load_b2(nxt // ZG)
-            if live(i - 3):
-                for c in range(2):
-                    pa(i - 3, c)
-                    pb(i - 3, c)
-                store(i - 3)
-            if live(i):
+            if live(c - 3):
+                l2(c - 3, 0)
+                l2(c - 3, 1)
+                pa(c - 3, 0)
+                pa(c - 3, 1)
+            if live(c):
                 for k in range(3):
-                    ta(i, k)
-                    ev(i, k)
-            if live(i - 1):
-                l1(i - 1, 0)
-                l1(i - 1, 1)
-            if live(i):
-                for k in range(3, 5):
-                    ta(i, k)
-                    ev(i, k)
-            if live(i - 2):
-                th(i - 2, 0)
-                th(i - 2, 1)
-            if live(i - 1):
-                p1(i - 1, 0)
-                p1(i - 1, 1)
-            if live(i - 2):
-                p2(i - 2)
-                qh(i - 2)
-                l2(i - 2, 0)
-                l2(i - 2, 1)
-            if live(i):
-                qz(i)
-                qw(i)
+                    ev(c, k)
+            if live(c - 3):
+                th(c - 3, 0)
+            if live(c):
+                ta(c, 3)
+            if live(c - 3):
+                th(c - 3, 1)
+            if live(c):
+                ta(c, 4)
+            if live(c - 3):
+                pb(c - 3, 0)
+                pb(c - 3, 1)
+                store(c - 3)
+            if live(c):
+                ev(c, 3)
+                ev(c, 4)
+            if live(c - 2):
+                p2(c - 2)
+            if live(c - 1):
+                l1(c - 1, 0)
+                l1(c - 1, 1)
+            if live(c - 2):
+                qh(c - 2)
+            if live(c):
+                qz(c)
+                qw(c, 0)
+                qw(c, 1)
+            if live(c - 1):
+                p1(c - 1, 0)
+                p1(c - 1, 1)
+            if live(c + 1):
+                for k in range(3):
+                    ta(c + 1, k)

@@ -13,8 +13,8 @@ ACT = mybir.ActivationFunctionType
 
 P = 128
 B, G, H = 256, 16, 512
-ZG = 4
-PRE = 4
+PRE = 8
+Z_GROUPS = ((0, 2), (2, 2), (4, 4), (8, 4), (12, 4))
 FLOPS = 2 * B * H * H * G * 2
 
 
@@ -22,8 +22,7 @@ def tile_linearwdecoder_pa_kernel(tc, z1, z2, W1, b1, W2, b2, out):
     nc = tc.nc
     with ExitStack() as ctx:
         const = ctx.enter_context(tc.tile_pool(name="const", bufs=1))
-        zpool = ctx.enter_context(tc.tile_pool(name="zpool", bufs=4))
-        wpool = ctx.enter_context(tc.tile_pool(name="wpool", bufs=6))
+        wpool = ctx.enter_context(tc.tile_pool(name="wpool", bufs=PRE + 2))
         gpool = ctx.enter_context(tc.tile_pool(name="gpool", bufs=2))
         cpool = ctx.enter_context(tc.tile_pool(name="cpool", bufs=3))
         hpool = ctx.enter_context(tc.tile_pool(name="hpool", bufs=3))
@@ -31,102 +30,128 @@ def tile_linearwdecoder_pa_kernel(tc, z1, z2, W1, b1, W2, b2, out):
         psum = ctx.enter_context(tc.psum_pool(name="psum", bufs=8))
         ctx.enter_context(tc.manual_schedule())
 
-        zraws = {}
+        zwords = {}
         st = {}
-        for g in range(G):
+        for g in range(G + 2):
             st[g] = {}
 
-        b2bc = const.tile([P, G * H], BF16)
-
-        def load_b2(q):
-            nc.sync.dma_start(
-                out=b2bc[:, q * ZG * H:(q + 1) * ZG * H],
-                in_=b2[q * ZG:(q + 1) * ZG, :].rearrange("g m -> (g m)").partition_broadcast(P))
-
         def load_z(q):
-            zraw = zpool.tile([P, 4096], BF16, tag="zraw")
+            first, n = Z_GROUPS[q]
+            zraw = const.tile([P, 4 * n * 256], BF16, name="zraw%d" % q)
             for u, src in enumerate((z1, z2)):
                 nc.sync.dma_start(
-                    out=zraw[:, u * 2048:(u + 1) * 2048].rearrange("p (c k) -> p c k", c=2),
-                    in_=src[:, q * 1024:(q + 1) * 1024].rearrange("(c p) k -> p c k", p=P))
-            zraws[q] = zraw
+                    out=zraw[:, u * n * 512:(u + 1) * n * 512].rearrange("p (c k) -> p c k", c=2),
+                    in_=src[:, first * 256:(first + n) * 256].rearrange("(c p) k -> p c k", p=P))
+            for g in range(first, first + n):
+                zwords[g] = (zraw, [(u * 2 + c) * n * P + (g - first) * P
+                                    for u in range(2) for c in range(2)])
 
         def load_w(g):
             wraw = wpool.tile([P, 4096], BF16, tag="wraw")
             for i, src in enumerate((W1, W2)):
-                nc.sync.dma_start(
-                    out=wraw[:, i * 2048:(i + 1) * 2048].rearrange("p (u c) -> p u c", u=2),
-                    in_=src[g].rearrange("(u j e) k -> j u (e k)", u=2, e=2))
+                nc.sync.dma_start(out=wraw[:, i * 2048:(i + 1) * 2048],
+                                  in_=src[g].rearrange("(j c) k -> j (c k)", c=4))
             st[g]["wraw"] = wraw
 
         braw = const.tile([P, 256], BF16)
         nc.vector.memset(braw[:], 0.0)
+        b2raw = const.tile([P, H], BF16)
+        nc.vector.memset(b2raw[:], 0.0)
         nc.sync.dma_start(out=braw[0:32, :], in_=b1.rearrange("g (u c) -> (g u) c", u=2))
+        nc.sync.dma_start(out=b2raw[0:G, :], in_=b2)
         load_z(0)
         load_w(0)
         load_w(1)
+        load_z(1)
         load_w(2)
-        load_b2(0)
         load_w(3)
+        load_z(2)
+        for g in range(4, PRE):
+            load_w(g)
 
         ident = const.tile([P, P], F32)
         make_identity(nc, ident[:])
         bsplit = const.tile([P, 2, P], F32)
         nc.vector.tensor_copy(out=bsplit[:], in_=braw[:].rearrange("r (p e) -> r e p", e=2))
+        sel = const.tile([P, G, P], BF16)
+        nc.vector.tensor_copy(out=sel[:], in_=ident[:, 0:G].unsqueeze(2).to_broadcast([P, G, P]))
         b1T = const.tile([P, 2, 32], F32)
         bt = psum.tile([P, 512], F32, tag="ps")
         for e in range(2):
             nc.tensor.transpose(bt[:, e * P:(e + 1) * P], bsplit[:, e, :], ident[:])
         nc.vector.tensor_copy(
             out=b1T[:], in_=bt[:, 0:256].rearrange("p (e r) -> p e r", e=2)[:, :, 0:32])
+        b2bc = const.tile([P, G * H], BF16)
+        b2banks = {}
+
+        def b2m(g):
+            bank = psum.tile([P, 512], F32, tag="ps")
+            nc.tensor.matmul(out=bank[:], lhsT=sel[:, g, :], rhs=b2raw[:], start=True, stop=True)
+            b2banks[g] = bank
+
+        def b2e(g):
+            nc.vector.tensor_copy(out=b2bc[:, g * H:(g + 1) * H], in_=b2banks[g][:])
 
         def ta(g, k):
             s = st[g]
             bank = psum.tile([P, 512], F32, tag="ps")
             if k == 0:
-                words = zraws[g // ZG][:].bitcast(F32)
-                offs = [(u * 2 + c) * 512 + (g % ZG) * P for u in range(2) for c in range(2)]
+                words = zwords[g][0][:].bitcast(F32)
+                offs = zwords[g][1]
             else:
                 words = s["wraw"][:].bitcast(F32)
-                v = k - 1
-                chunks = [2 * v, 2 * v + 1] if v < 2 else [4 + (v - 2), 6 + (v - 2)]
-                offs = [chunks[half] * 256 + uw * P for uw in range(2) for half in range(2)]
+                if k < 3:
+                    offs = [(2 * ch + k - 1) * 256 + uw * P for ch in range(2) for uw in range(2)]
+                else:
+                    offs = [1024 + (2 * (k - 3) + half) * 256 + uw * P
+                            for uw in range(2) for half in range(2)]
             for n, o in enumerate(offs):
                 nc.tensor.transpose(bank[:, n * P:(n + 1) * P], words[:, o:o + P], ident[:])
             s["bank%d" % k] = bank
 
         def ev(g, k):
             s = st[g]
+            bank = s["bank%d" % k]
             if k == 0:
-                grz = gpool.tile([P, 1024], BF16, tag="grz", align_bytes=64)
-                s["grz"] = grz
-                dst = grz[:].bitcast(F32)
-            else:
+                gzh = gpool.tile([P, 2048], BF16, tag="gzh", align_bytes=64)
+                s["gzh"] = gzh
+                dst = gzh[:].bitcast(F32)[:, 0:512].rearrange("p (c u) -> p c u", u=2)
+                src = bank[:].rearrange("p (u c) -> p c u", u=2)
+            elif k < 3:
                 if k == 1:
                     grw = gpool.tile([P, 4096], BF16, tag="grw", align_bytes=64)
                     s["grw"] = grw
-                dst = s["grw"][:].bitcast(F32)[:, (k - 1) * 512:k * 512]
-            nc.scalar.copy(out=dst.rearrange("p (c u) -> p c u", u=2),
-                           in_=s["bank%d" % k][:].rearrange("p (u c) -> p c u", u=2))
+                dst = s["grw"][:].bitcast(F32)[:, 0:1024].rearrange(
+                    "p (u e j q) -> p e u j q", u=2, e=2, q=4)[:, k - 1]
+                src = bank[:].rearrange("p (q u j) -> p u j q", q=4, u=2)
+            else:
+                dst = s["grw"][:].bitcast(F32)[:, (k - 1) * 512:k * 512].rearrange(
+                    "p (c u) -> p c u", u=2)
+                src = bank[:].rearrange("p (u c) -> p c u", u=2)
+            nc.scalar.copy(out=dst, in_=src)
 
-        def qz(g):
-            s = st[g]
-            cz = cpool.tile([P, 256], U32, tag="cz", align_bytes=64)
-            sz = cpool.tile([P, 256], U8, tag="sz", align_bytes=64)
-            nc.vector.quantize_mx(out=cz[:].bitcast(FP8X4), scales=sz[:], in_=s["grz"][:])
-            s["cz"] = cz
-            s["sz"] = sz
+        def qzh(c):
+            lo = 0 if c < G else 1
+            hi = 2 if c >= 2 else 1
+            czh = cpool.tile([P, 512], U32, tag="czh", align_bytes=64)
+            szh = cpool.tile([P, 512], U8, tag="szh", align_bytes=64)
+            nc.vector.quantize_mx(out=czh[:, lo * 256:hi * 256].bitcast(FP8X4),
+                                  scales=szh[:, lo * 256:hi * 256],
+                                  in_=st[c]["gzh"][:, lo * 1024:hi * 1024])
+            if c < G:
+                st[c]["cz"] = czh[:, 0:256]
+                st[c]["sz"] = szh[:, 0:256]
+            if c >= 2:
+                st[c - 2]["ch"] = czh[:, 256:512]
+                st[c - 2]["sh"] = szh[:, 256:512]
 
-        def qw(g, i):
+        def qw(g):
             s = st[g]
-            if i == 0:
-                cw = cpool.tile([P, 1024], U32, tag="cw", align_bytes=64)
-                sw = cpool.tile([P, 1024], U8, tag="sw", align_bytes=64)
-                s["cw"] = cw
-                s["sw"] = sw
-            nc.vector.quantize_mx(out=s["cw"][:, i * 512:(i + 1) * 512].bitcast(FP8X4),
-                                  scales=s["sw"][:, i * 512:(i + 1) * 512],
-                                  in_=s["grw"][:, i * 2048:(i + 1) * 2048])
+            cw = cpool.tile([P, 1024], U32, tag="cw", align_bytes=64)
+            sw = cpool.tile([P, 1024], U8, tag="sw", align_bytes=64)
+            nc.vector.quantize_mx(out=cw[:].bitcast(FP8X4), scales=sw[:], in_=s["grw"][:])
+            s["cw"] = cw
+            s["sw"] = sw
 
         def l1(g, v):
             s = st[g]
@@ -137,7 +162,7 @@ def tile_linearwdecoder_pa_kernel(tc, z1, z2, W1, b1, W2, b2, out):
                     out=y1[:, half * 256:(half + 1) * 256],
                     lhsT=s["cw"][:, t * P:(t + 1) * P].bitcast(FP8X4),
                     lhsT_scale=s["sw"][:, t * P:(t + 1) * P],
-                    rhs=s["cz"][:].bitcast(FP8X4), rhs_scale=s["sz"][:],
+                    rhs=s["cz"].bitcast(FP8X4), rhs_scale=s["sz"],
                     start=True, stop=True)
             s["y1_%d" % v] = y1
 
@@ -153,21 +178,13 @@ def tile_linearwdecoder_pa_kernel(tc, z1, z2, W1, b1, W2, b2, out):
                     bias=b1T[:, half, 2 * g + v:2 * g + v + 1], scale=1.0)
 
         def p2(g):
-            s = st[g]
-            grh = gpool.tile([P, 1024], BF16, tag="grh", align_bytes=64)
+            if g + 2 >= G:
+                gzh = gpool.tile([P, 2048], BF16, tag="gzh", align_bytes=64)
+                st[g + 2]["gzh"] = gzh
             nc.gpsimd.tensor_scalar(
-                out=grh[:].rearrange("p (b t) -> p b t", t=4),
-                in0=s["h1T"][:].rearrange("p t b -> p b t"),
+                out=st[g + 2]["gzh"][:, 1024:2048].rearrange("p (b t) -> p b t", t=4),
+                in0=st[g]["h1T"][:].rearrange("p t b -> p b t"),
                 scalar1=1.0, scalar2=0.0, op0=ALU.mult, op1=ALU.add)
-            s["grh"] = grh
-
-        def qh(g):
-            s = st[g]
-            ch = cpool.tile([P, 256], U32, tag="ch", align_bytes=64)
-            sh = cpool.tile([P, 256], U8, tag="sh", align_bytes=64)
-            nc.vector.quantize_mx(out=ch[:].bitcast(FP8X4), scales=sh[:], in_=s["grh"][:])
-            s["ch"] = ch
-            s["sh"] = sh
 
         def th(g, c):
             s = st[g]
@@ -193,75 +210,106 @@ def tile_linearwdecoder_pa_kernel(tc, z1, z2, W1, b1, W2, b2, out):
             s = st[g]
             tmp = opool.tile([P, H], F32, tag="tmp")
             nc.vector.tensor_tensor(
-                out=tmp[:].rearrange("p (j e) -> p j e", e=2),
-                in0=s["y2_%d" % c][:].rearrange("p (e j) -> p j e", e=2),
-                in1=b2bc[:, g * H:(g + 1) * H].rearrange("p (j e) -> p j e", e=2),
+                out=tmp[:].rearrange("p (j r) -> p j r", r=4),
+                in0=s["y2_%d" % c][:].rearrange("p (r j) -> p j r", r=4),
+                in1=b2bc[:, g * H:(g + 1) * H].rearrange("p (j r) -> p j r", r=4),
                 op=ALU.add)
             s["tmp%d" % c] = tmp
 
         def pb(g, c):
             s = st[g]
-            if c == 0:
-                osb = opool.tile([P, 2, H], F32, tag="osb")
+            if c == 0 and g % 2 == 0:
+                osb = opool.tile([P, 2, 2, H], F32, tag="osb")
                 s["osb"] = osb
+                st[g + 1]["osb"] = osb
             nc.vector.scalar_tensor_tensor(
-                out=s["osb"][:, c, :].rearrange("p (j e) -> p j e", e=2),
+                out=s["osb"][:, c, g % 2, :].rearrange("p (j e) -> p j e", e=2),
                 in0=s["tmp%d" % c][:].rearrange("p (j e) -> p j e", e=2),
                 scalar=0.0,
                 in1=s["hn%d" % c][:].rearrange("p (e j) -> p j e", e=2),
                 op0=ALU.max, op1=ALU.add)
 
-        def store(g):
+        def store_pair(g):
+            nc.sync.dma_start(
+                out=out[:, g - 1:g + 1, :].rearrange("(c p) g m -> p c (g m)", p=P),
+                in_=st[g]["osb"][:].rearrange("p c g m -> p c (g m)"))
+
+        def store_code(g):
             nc.sync.dma_start(out=out[:, g, :].rearrange("(c p) m -> p c m", p=P),
-                              in_=st[g]["osb"][:])
+                              in_=st[g]["osb"][:, :, g % 2, :])
+
+        def store_half(g, c):
+            nc.sync.dma_start(out=out[c * P:(c + 1) * P, g, :], in_=st[g]["osb"][:, c, g % 2, :])
 
         def live(g):
             return 0 <= g < G
 
+        for g in range(4):
+            b2m(g)
+            b2e(g)
         for k in range(3):
             ta(0, k)
         for c in range(G + 3):
             nxt = c + PRE
+            x = c - 3
+            fill = 4 + 4 * c
             if nxt < G:
-                if nxt % ZG == 0:
-                    load_z(nxt // ZG)
+                if nxt % 4 == 0:
+                    load_z(nxt // 4 + 1)
                 load_w(nxt)
-                if nxt % ZG == 1:
-                    load_b2(nxt // ZG)
-            if live(c - 3):
-                l2(c - 3, 0)
-                l2(c - 3, 1)
-                pa(c - 3, 0)
-                pa(c - 3, 1)
+            if c < 3:
+                b2m(fill)
+                b2m(fill + 1)
+                b2e(fill)
+                b2e(fill + 1)
+            if live(x):
+                l2(x, 0)
+                l2(x, 1)
+                pa(x, 0)
+                pa(x, 1)
+            if c >= G and live(c - 2):
+                p2(c - 2)
+                qzh(c)
             if live(c):
                 for k in range(3):
                     ev(c, k)
-            if live(c - 3):
-                th(c - 3, 0)
+            if c < 3:
+                b2m(fill + 2)
+            if live(x):
+                th(x, 0)
             if live(c):
                 ta(c, 3)
-            if live(c - 3):
-                th(c - 3, 1)
+            if c < 3:
+                b2m(fill + 3)
+            if live(x):
+                th(x, 1)
             if live(c):
                 ta(c, 4)
-            if live(c - 3):
-                pb(c - 3, 0)
-                pb(c - 3, 1)
-                store(c - 3)
+            if c < 3:
+                b2e(fill + 2)
+                b2e(fill + 3)
+            if live(x):
+                pb(x, 0)
+                if x == G - 1:
+                    store_half(x, 0)
+                pb(x, 1)
+                if x == G - 1:
+                    store_half(x, 1)
+                elif x == G - 2:
+                    store_code(x)
+                elif x % 2 == 1:
+                    store_pair(x)
             if live(c):
                 ev(c, 3)
                 ev(c, 4)
-            if live(c - 2):
+            if c < G and live(c - 2):
                 p2(c - 2)
             if live(c - 1):
                 l1(c - 1, 0)
                 l1(c - 1, 1)
-            if live(c - 2):
-                qh(c - 2)
-            if live(c):
-                qz(c)
-                qw(c, 0)
-                qw(c, 1)
+            if c < G:
+                qzh(c)
+                qw(c)
             if live(c - 1):
                 p1(c - 1, 0)
                 p1(c - 1, 1)

@@ -13,7 +13,7 @@ ACT = mybir.ActivationFunctionType
 
 P = 128
 B, G, H = 256, 16, 512
-PRE = 8
+PRE = 6
 Z_GROUPS = ((0, 2), (2, 2), (4, 4), (8, 4), (12, 4))
 FLOPS = 2 * B * H * H * G * 2
 
@@ -27,6 +27,7 @@ def tile_linearwdecoder_pa_kernel(tc, z1, z2, W1, b1, W2, b2, out):
         cpool = ctx.enter_context(tc.tile_pool(name="cpool", bufs=3))
         hpool = ctx.enter_context(tc.tile_pool(name="hpool", bufs=3))
         opool = ctx.enter_context(tc.tile_pool(name="opool", bufs=3))
+        spool = ctx.enter_context(tc.tile_pool(name="spool", bufs=4))
         psum = ctx.enter_context(tc.psum_pool(name="psum", bufs=8))
         ctx.enter_context(tc.manual_schedule())
 
@@ -219,7 +220,7 @@ def tile_linearwdecoder_pa_kernel(tc, z1, z2, W1, b1, W2, b2, out):
         def pb(g, c):
             s = st[g]
             if c == 0 and g % 2 == 0:
-                osb = opool.tile([P, 2, 2, H], F32, tag="osb")
+                osb = spool.tile([P, 2, 2, H], F32, tag="osb")
                 s["osb"] = osb
                 st[g + 1]["osb"] = osb
             nc.vector.scalar_tensor_tensor(

@@ -85,13 +85,15 @@ def tile_linearwdecoder_pa_kernel(tc, z1, z2, W1, b1, W2, b2, out):
         b2bc = const.tile([P, G * H], BF16)
         b2banks = {}
 
-        def b2m(g):
-            bank = psum.tile([P, 512], F32, tag="ps")
-            nc.tensor.matmul(out=bank[:], lhsT=sel[:, g, :], rhs=b2raw[:], start=True, stop=True)
-            b2banks[g] = bank
+        def b2m(i):
+            bank = psum.tile([P, 2 * H], BF16, tag="ps")
+            for n in range(2):
+                nc.tensor.matmul(out=bank[:, n * H:(n + 1) * H], lhsT=sel[:, 2 * i + n, :],
+                                 rhs=b2raw[:], start=True, stop=True)
+            b2banks[i] = bank
 
-        def b2e(g):
-            nc.vector.tensor_copy(out=b2bc[:, g * H:(g + 1) * H], in_=b2banks[g][:])
+        def b2e(i):
+            nc.vector.tensor_copy(out=b2bc[:, 2 * i * H:2 * (i + 1) * H], in_=b2banks[i][:])
 
         def ta(g, k):
             s = st[g]
@@ -219,12 +221,18 @@ def tile_linearwdecoder_pa_kernel(tc, z1, z2, W1, b1, W2, b2, out):
 
         def pb(g, c):
             s = st[g]
-            if c == 0 and g % 2 == 0:
-                osb = spool.tile([P, 2, 2, H], F32, tag="osb")
-                s["osb"] = osb
-                st[g + 1]["osb"] = osb
+            if g >= G - 2:
+                osl = spool.tile([P, H], F32, tag="osl")
+                s["osl%d" % c] = osl
+                dst = osl[:]
+            else:
+                if c == 0 and g % 2 == 0:
+                    osb = spool.tile([P, 2, 2, H], F32, tag="osb")
+                    s["osb"] = osb
+                    st[g + 1]["osb"] = osb
+                dst = s["osb"][:, c, g % 2, :]
             nc.vector.scalar_tensor_tensor(
-                out=s["osb"][:, c, g % 2, :].rearrange("p (j e) -> p j e", e=2),
+                out=dst.rearrange("p (j e) -> p j e", e=2),
                 in0=s["tmp%d" % c][:].rearrange("p (j e) -> p j e", e=2),
                 scalar=0.0,
                 in1=s["hn%d" % c][:].rearrange("p (e j) -> p j e", e=2),
@@ -235,34 +243,28 @@ def tile_linearwdecoder_pa_kernel(tc, z1, z2, W1, b1, W2, b2, out):
                 out=out[:, g - 1:g + 1, :].rearrange("(c p) g m -> p c (g m)", p=P),
                 in_=st[g]["osb"][:].rearrange("p c g m -> p c (g m)"))
 
-        def store_code(g):
-            nc.sync.dma_start(out=out[:, g, :].rearrange("(c p) m -> p c m", p=P),
-                              in_=st[g]["osb"][:, :, g % 2, :])
-
         def store_half(g, c):
-            nc.sync.dma_start(out=out[c * P:(c + 1) * P, g, :], in_=st[g]["osb"][:, c, g % 2, :])
+            nc.sync.dma_start(out=out[c * P:(c + 1) * P, g, :], in_=st[g]["osl%d" % c][:])
 
         def live(g):
             return 0 <= g < G
 
-        for g in range(4):
-            b2m(g)
-            b2e(g)
+        for i in range(2):
+            b2m(i)
+            b2e(i)
         for k in range(3):
             ta(0, k)
         for c in range(G + 3):
             nxt = c + PRE
             x = c - 3
-            fill = 4 + 4 * c
+            fill = 2 + 2 * c
             if nxt < G:
                 if nxt % 4 == 0:
                     load_z(nxt // 4 + 1)
                 load_w(nxt)
             if c < 3:
                 b2m(fill)
-                b2m(fill + 1)
                 b2e(fill)
-                b2e(fill + 1)
             if live(x):
                 l2(x, 0)
                 l2(x, 1)
@@ -275,29 +277,24 @@ def tile_linearwdecoder_pa_kernel(tc, z1, z2, W1, b1, W2, b2, out):
                 for k in range(3):
                     ev(c, k)
             if c < 3:
-                b2m(fill + 2)
+                b2m(fill + 1)
             if live(x):
                 th(x, 0)
             if live(c):
                 ta(c, 3)
-            if c < 3:
-                b2m(fill + 3)
             if live(x):
                 th(x, 1)
             if live(c):
                 ta(c, 4)
             if c < 3:
-                b2e(fill + 2)
-                b2e(fill + 3)
+                b2e(fill + 1)
             if live(x):
                 pb(x, 0)
-                if x == G - 1:
+                if x >= G - 2:
                     store_half(x, 0)
                 pb(x, 1)
-                if x == G - 1:
+                if x >= G - 2:
                     store_half(x, 1)
-                elif x == G - 2:
-                    store_code(x)
                 elif x % 2 == 1:
                     store_pair(x)
             if live(c):

@@ -13,6 +13,7 @@ ACT = mybir.ActivationFunctionType
 
 P = 128
 B, G, H = 256, 16, 512
+Q_END = 12
 PRE = 6
 Z_GROUPS = ((0, 2), (2, 2), (4, 4), (8, 4), (12, 4))
 FLOPS = 2 * B * H * H * G * 2
@@ -22,10 +23,11 @@ def tile_linearwdecoder_pa_kernel(tc, z1, z2, W1, b1, W2, b2, out):
     nc = tc.nc
     with ExitStack() as ctx:
         const = ctx.enter_context(tc.tile_pool(name="const", bufs=1))
-        wpool = ctx.enter_context(tc.tile_pool(name="wpool", bufs=PRE + 2))
+        wpool = ctx.enter_context(tc.tile_pool(name="wpool", bufs=PRE + 1))
         gpool = ctx.enter_context(tc.tile_pool(name="gpool", bufs=2))
         cpool = ctx.enter_context(tc.tile_pool(name="cpool", bufs=3))
         hpool = ctx.enter_context(tc.tile_pool(name="hpool", bufs=3))
+        qopool = ctx.enter_context(tc.tile_pool(name="qopool", bufs=3))
         opool = ctx.enter_context(tc.tile_pool(name="opool", bufs=3))
         spool = ctx.enter_context(tc.tile_pool(name="spool", bufs=4))
         psum = ctx.enter_context(tc.psum_pool(name="psum", bufs=8))
@@ -95,9 +97,12 @@ def tile_linearwdecoder_pa_kernel(tc, z1, z2, W1, b1, W2, b2, out):
         def b2e(i):
             nc.vector.tensor_copy(out=b2bc[:, 2 * i * H:2 * (i + 1) * H], in_=b2banks[i][:])
 
-        def ta(g, k):
+        def ta(g, k, lo=0, hi=4):
             s = st[g]
-            bank = psum.tile([P, 512], F32, tag="ps")
+            if lo == 0:
+                bank = psum.tile([P, 512], F32, tag="ps")
+                s["bank%d" % k] = bank
+            bank = s["bank%d" % k]
             if k == 0:
                 words = zwords[g][0][:].bitcast(F32)
                 offs = zwords[g][1]
@@ -108,9 +113,9 @@ def tile_linearwdecoder_pa_kernel(tc, z1, z2, W1, b1, W2, b2, out):
                 else:
                     offs = [1024 + (2 * (k - 3) + half) * 256 + uw * P
                             for uw in range(2) for half in range(2)]
-            for n, o in enumerate(offs):
+            for n in range(lo, hi):
+                o = offs[n]
                 nc.tensor.transpose(bank[:, n * P:(n + 1) * P], words[:, o:o + P], ident[:])
-            s["bank%d" % k] = bank
 
         def ev(g, k):
             s = st[g]
@@ -189,14 +194,16 @@ def tile_linearwdecoder_pa_kernel(tc, z1, z2, W1, b1, W2, b2, out):
                 in0=st[g]["h1T"][:].rearrange("p t b -> p b t"),
                 scalar1=1.0, scalar2=0.0, op0=ALU.mult, op1=ALU.add)
 
-        def th(g, c):
+        def th(g, c, lo=0, hi=4):
             s = st[g]
-            hn = psum.tile([P, 512], F32, tag="ps")
-            for t in range(4):
+            if lo == 0:
+                hn = psum.tile([P, 512], F32, tag="ps")
+                s["hn%d" % c] = hn
+            hn = s["hn%d" % c]
+            for t in range(lo, hi):
                 pos = 2 * (t % 2) + t // 2
                 nc.tensor.transpose(hn[:, pos * P:(pos + 1) * P],
                                     s["h1T"][:, t, c * P:(c + 1) * P], ident[:])
-            s["hn%d" % c] = hn
 
         def l2(g, c):
             s = st[g]
@@ -221,13 +228,19 @@ def tile_linearwdecoder_pa_kernel(tc, z1, z2, W1, b1, W2, b2, out):
 
         def pb(g, c):
             s = st[g]
-            if g >= G - 2:
+            if g < Q_END:
+                if c == 0 and g % 4 == 0:
+                    osq = qopool.tile([P, 2, 4, H], F32, tag="osq")
+                    for i in range(4):
+                        st[g + i]["osq"] = osq
+                dst = st[g]["osq"][:, c, g % 4, :]
+            elif g >= G - 2:
                 osl = spool.tile([P, H], F32, tag="osl")
                 s["osl%d" % c] = osl
                 dst = osl[:]
             else:
                 if c == 0 and g % 2 == 0:
-                    osb = spool.tile([P, 2, 2, H], F32, tag="osb")
+                    osb = qopool.tile([P, 2, 2, H], F32, tag="osq")
                     s["osb"] = osb
                     st[g + 1]["osb"] = osb
                 dst = s["osb"][:, c, g % 2, :]
@@ -242,6 +255,11 @@ def tile_linearwdecoder_pa_kernel(tc, z1, z2, W1, b1, W2, b2, out):
             nc.sync.dma_start(
                 out=out[:, g - 1:g + 1, :].rearrange("(c p) g m -> p c (g m)", p=P),
                 in_=st[g]["osb"][:].rearrange("p c g m -> p c (g m)"))
+
+        def store_group(g):
+            nc.sync.dma_start(
+                out=out[:, g - 3:g + 1, :].rearrange("(c p) g m -> p c (g m)", p=P),
+                in_=st[g]["osq"][:].rearrange("p c g m -> p c (g m)"))
 
         def store_half(g, c):
             nc.sync.dma_start(out=out[c * P:(c + 1) * P, g, :], in_=st[g]["osl%d" % c][:])
@@ -295,6 +313,9 @@ def tile_linearwdecoder_pa_kernel(tc, z1, z2, W1, b1, W2, b2, out):
                 pb(x, 1)
                 if x >= G - 2:
                     store_half(x, 1)
+                elif x < Q_END:
+                    if x % 4 == 3:
+                        store_group(x)
                 elif x % 2 == 1:
                     store_pair(x)
             if live(c):

from contextlib import ExitStack

import concourse.mybir as mybir
from concourse.masks import make_identity

F32 = mybir.dt.float32
BF16 = mybir.dt.bfloat16
U32 = mybir.dt.uint32
U8 = mybir.dt.uint8
FP8X4 = mybir.dt.float8_e4m3fn_x4
ALU = mybir.AluOpType
ACT = mybir.ActivationFunctionType

P = 128
B, G, H = 256, 16, 512
Q_END = 12
PRE = 6
Z_GROUPS = ((0, 2), (2, 2), (4, 4), (8, 4), (12, 4))
FLOPS = 2 * B * H * H * G * 2


def tile_linearwdecoder_pa_kernel(tc, z1, z2, W1, b1, W2, b2, out):
    nc = tc.nc
    with ExitStack() as ctx:
        const = ctx.enter_context(tc.tile_pool(name="const", bufs=1))
        wpool = ctx.enter_context(tc.tile_pool(name="wpool", bufs=PRE + 1))
        gpool = ctx.enter_context(tc.tile_pool(name="gpool", bufs=2))
        cpool = ctx.enter_context(tc.tile_pool(name="cpool", bufs=3))
        hpool = ctx.enter_context(tc.tile_pool(name="hpool", bufs=3))
        qopool = ctx.enter_context(tc.tile_pool(name="qopool", bufs=3))
        opool = ctx.enter_context(tc.tile_pool(name="opool", bufs=3))
        spool = ctx.enter_context(tc.tile_pool(name="spool", bufs=4))
        psum = ctx.enter_context(tc.psum_pool(name="psum", bufs=8))
        ctx.enter_context(tc.manual_schedule())

        zwords = {}
        st = {}
        for g in range(G + 2):
            st[g] = {}

        def load_z(q):
            first, n = Z_GROUPS[q]
            zraw = const.tile([P, 4 * n * 256], BF16, name="zraw%d" % q)
            for u, src in enumerate((z1, z2)):
                nc.sync.dma_start(
                    out=zraw[:, u * n * 512:(u + 1) * n * 512].rearrange("p (c k) -> p c k", c=2),
                    in_=src[:, first * 256:(first + n) * 256].rearrange("(c p) k -> p c k", p=P))
            for g in range(first, first + n):
                zwords[g] = (zraw, [(u * 2 + c) * n * P + (g - first) * P
                                    for u in range(2) for c in range(2)])

        def load_w(g):
            wraw = wpool.tile([P, 4096], BF16, tag="wraw")
            for i, src in enumerate((W1, W2)):
                nc.sync.dma_start(out=wraw[:, i * 2048:(i + 1) * 2048],
                                  in_=src[g].rearrange("(j c) k -> j (c k)", c=4))
            st[g]["wraw"] = wraw

        braw = const.tile([P, 256], BF16)
        nc.vector.memset(braw[:], 0.0)
        b2raw = const.tile([P, H], BF16)
        nc.vector.memset(b2raw[:], 0.0)
        nc.sync.dma_start(out=braw[0:32, :], in_=b1.rearrange("g (u c) -> (g u) c", u=2))
        nc.sync.dma_start(out=b2raw[0:G, :], in_=b2)
        load_z(0)
        load_w(0)
        load_w(1)
        load_z(1)
        load_w(2)
        load_w(3)
        load_z(2)
        for g in range(4, PRE):
            load_w(g)

        ident = const.tile([P, P], F32)
        make_identity(nc, ident[:])
        bsplit = const.tile([P, 2, P], F32)
        nc.vector.tensor_copy(out=bsplit[:], in_=braw[:].rearrange("r (p e) -> r e p", e=2))
        sel = const.tile([P, G, P], BF16)
        nc.vector.tensor_copy(out=sel[:], in_=ident[:, 0:G].unsqueeze(2).to_broadcast([P, G, P]))
        b1T = const.tile([P, 2, 32], F32)
        bt = psum.tile([P, 512], F32, tag="ps")
        for e in range(2):
            nc.tensor.transpose(bt[:, e * P:(e + 1) * P], bsplit[:, e, :], ident[:])
        nc.vector.tensor_copy(
            out=b1T[:], in_=bt[:, 0:256].rearrange("p (e r) -> p e r", e=2)[:, :, 0:32])
        b2bc = const.tile([P, G * H], BF16)
        b2banks = {}

        def b2m(i):
            bank = psum.tile([P, 2 * H], BF16, tag="ps")
            for n in range(2):
                nc.tensor.matmul(out=bank[:, n * H:(n + 1) * H], lhsT=sel[:, 2 * i + n, :],
                                 rhs=b2raw[:], start=True, stop=True)
            b2banks[i] = bank

        def b2e(i):
            nc.vector.tensor_copy(out=b2bc[:, 2 * i * H:2 * (i + 1) * H], in_=b2banks[i][:])

        def ta(g, k, lo=0, hi=4):
            s = st[g]
            if lo == 0:
                bank = psum.tile([P, 512], F32, tag="ps")
                s["bank%d" % k] = bank
            bank = s["bank%d" % k]
            if k == 0:
                words = zwords[g][0][:].bitcast(F32)
                offs = zwords[g][1]
            else:
                words = s["wraw"][:].bitcast(F32)
                if k < 3:
                    offs = [(2 * ch + k - 1) * 256 + uw * P for ch in range(2) for uw in range(2)]
                else:
                    offs = [1024 + (2 * (k - 3) + half) * 256 + uw * P
                            for uw in range(2) for half in range(2)]
            for n in range(lo, hi):
                o = offs[n]
                nc.tensor.transpose(bank[:, n * P:(n + 1) * P], words[:, o:o + P], ident[:])

        def ev(g, k):
            s = st[g]
            bank = s["bank%d" % k]
            if k == 0:
                gzh = gpool.tile([P, 2048], BF16, tag="gzh", align_bytes=64)
                s["gzh"] = gzh
                dst = gzh[:].bitcast(F32)[:, 0:512].rearrange("p (c u) -> p c u", u=2)
                src = bank[:].rearrange("p (u c) -> p c u", u=2)
            elif k < 3:
                if k == 1:
                    grw = gpool.tile([P, 4096], BF16, tag="grw", align_bytes=64)
                    s["grw"] = grw
                dst = s["grw"][:].bitcast(F32)[:, 0:1024].rearrange(
                    "p (u e j q) -> p e u j q", u=2, e=2, q=4)[:, k - 1]
                src = bank[:].rearrange("p (q u j) -> p u j q", q=4, u=2)
            else:
                dst = s["grw"][:].bitcast(F32)[:, (k - 1) * 512:k * 512].rearrange(
                    "p (c u) -> p c u", u=2)
                src = bank[:].rearrange("p (u c) -> p c u", u=2)
            nc.scalar.copy(out=dst, in_=src)

        def qzh(c):
            lo = 0 if c < G else 1
            hi = 2 if c >= 2 else 1
            czh = cpool.tile([P, 512], U32, tag="czh", align_bytes=64)
            szh = cpool.tile([P, 512], U8, tag="szh", align_bytes=64)
            nc.vector.quantize_mx(out=czh[:, lo * 256:hi * 256].bitcast(FP8X4),
                                  scales=szh[:, lo * 256:hi * 256],
                                  in_=st[c]["gzh"][:, lo * 1024:hi * 1024])
            if c < G:
                st[c]["cz"] = czh[:, 0:256]
                st[c]["sz"] = szh[:, 0:256]
            if c >= 2:
                st[c - 2]["ch"] = czh[:, 256:512]
                st[c - 2]["sh"] = szh[:, 256:512]

        def qw(g):
            s = st[g]
            cw = cpool.tile([P, 1024], U32, tag="cw", align_bytes=64)
            sw = cpool.tile([P, 1024], U8, tag="sw", align_bytes=64)
            nc.vector.quantize_mx(out=cw[:].bitcast(FP8X4), scales=sw[:], in_=s["grw"][:])
            s["cw"] = cw
            s["sw"] = sw

        def l1(g, v):
            s = st[g]
            y1 = psum.tile([P, 512], F32, tag="ps")
            for half in range(2):
                t = 2 * v + half
                nc.tensor.matmul_mx(
                    out=y1[:, half * 256:(half + 1) * 256],
                    lhsT=s["cw"][:, t * P:(t + 1) * P].bitcast(FP8X4),
                    lhsT_scale=s["sw"][:, t * P:(t + 1) * P],
                    rhs=s["cz"].bitcast(FP8X4), rhs_scale=s["sz"],
                    start=True, stop=True)
            s["y1_%d" % v] = y1

        def p1(g, v):
            s = st[g]
            if v == 0:
                h1T = hpool.tile([P, 4, 256], F32, tag="h1T")
                s["h1T"] = h1T
            for half in range(2):
                nc.scalar.activation(
                    out=s["h1T"][:, 2 * v + half, :],
                    in_=s["y1_%d" % v][:, half * 256:(half + 1) * 256], func=ACT.Relu,
                    bias=b1T[:, half, 2 * g + v:2 * g + v + 1], scale=1.0)

        def p2(g):
            if g + 2 >= G:
                gzh = gpool.tile([P, 2048], BF16, tag="gzh", align_bytes=64)
                st[g + 2]["gzh"] = gzh
            nc.gpsimd.tensor_scalar(
                out=st[g + 2]["gzh"][:, 1024:2048].rearrange("p (b t) -> p b t", t=4),
                in0=st[g]["h1T"][:].rearrange("p t b -> p b t"),
                scalar1=1.0, scalar2=0.0, op0=ALU.mult, op1=ALU.add)

        def th(g, c, lo=0, hi=4):
            s = st[g]
            if lo == 0:
                hn = psum.tile([P, 512], F32, tag="ps")
                s["hn%d" % c] = hn
            hn = s["hn%d" % c]
            for t in range(lo, hi):
                pos = 2 * (t % 2) + t // 2
                nc.tensor.transpose(hn[:, pos * P:(pos + 1) * P],
                                    s["h1T"][:, t, c * P:(c + 1) * P], ident[:])

        def l2(g, c):
            s = st[g]
            y2 = psum.tile([P, 512], F32, tag="ps")
            nc.tensor.matmul_mx(
                out=y2[:],
                lhsT=s["ch"][:, c * P:(c + 1) * P].bitcast(FP8X4),
                lhsT_scale=s["sh"][:, c * P:(c + 1) * P],
                rhs=s["cw"][:, 512:1024].bitcast(FP8X4), rhs_scale=s["sw"][:, 512:1024],
                start=True, stop=True)
            s["y2_%d" % c] = y2

        def pa(g, c):
            s = st[g]
            tmp = opool.tile([P, H], F32, tag="tmp")
            nc.vector.tensor_tensor(
                out=tmp[:].rearrange("p (j r) -> p j r", r=4),
                in0=s["y2_%d" % c][:].rearrange("p (r j) -> p j r", r=4),
                in1=b2bc[:, g * H:(g + 1) * H].rearrange("p (j r) -> p j r", r=4),
                op=ALU.add)
            s["tmp%d" % c] = tmp

        def pb(g, c):
            s = st[g]
            if g < Q_END:
                if c == 0 and g % 4 == 0:
                    osq = qopool.tile([P, 2, 4, H], F32, tag="osq")
                    for i in range(4):
                        st[g + i]["osq"] = osq
                dst = st[g]["osq"][:, c, g % 4, :]
            elif g >= G - 2:
                osl = spool.tile([P, H], F32, tag="osl")
                s["osl%d" % c] = osl
                dst = osl[:]
            else:
                if c == 0 and g % 2 == 0:
                    osb = qopool.tile([P, 2, 2, H], F32, tag="osq")
                    s["osb"] = osb
                    st[g + 1]["osb"] = osb
                dst = s["osb"][:, c, g % 2, :]
            nc.vector.scalar_tensor_tensor(
                out=dst.rearrange("p (j e) -> p j e", e=2),
                in0=s["tmp%d" % c][:].rearrange("p (j e) -> p j e", e=2),
                scalar=0.0,
                in1=s["hn%d" % c][:].rearrange("p (e j) -> p j e", e=2),
                op0=ALU.max, op1=ALU.add)

        def store_pair(g):
            nc.sync.dma_start(
                out=out[:, g - 1:g + 1, :].rearrange("(c p) g m -> p c (g m)", p=P),
                in_=st[g]["osb"][:].rearrange("p c g m -> p c (g m)"))

        def store_group(g):
            nc.sync.dma_start(
                out=out[:, g - 3:g + 1, :].rearrange("(c p) g m -> p c (g m)", p=P),
                in_=st[g]["osq"][:].rearrange("p c g m -> p c (g m)"))

        def store_half(g, c):
            nc.sync.dma_start(out=out[c * P:(c + 1) * P, g, :], in_=st[g]["osl%d" % c][:])

        def live(g):
            return 0 <= g < G

        for i in range(2):
            b2m(i)
            b2e(i)
        for k in range(3):
            ta(0, k)
        for c in range(G + 3):
            nxt = c + PRE
            x = c - 3
            fill = 2 + 2 * c
            if nxt < G:
                if nxt % 4 == 0:
                    load_z(nxt // 4 + 1)
                load_w(nxt)
            if c < 3:
                b2m(fill)
                b2e(fill)
            if live(x):
                l2(x, 0)
                l2(x, 1)
                pa(x, 0)
                pa(x, 1)
            if c >= G and live(c - 2):
                p2(c - 2)
                qzh(c)
            if live(c):
                for k in range(3):
                    ev(c, k)
            if c < 3:
                b2m(fill + 1)
            if live(x):
                th(x, 0)
            if live(c):
                ta(c, 3)
            if live(x):
                th(x, 1)
            if live(c):
                ta(c, 4)
            if c < 3:
                b2e(fill + 1)
            if live(x):
                pb(x, 0)
                if x >= G - 2:
                    store_half(x, 0)
                pb(x, 1)
                if x >= G - 2:
                    store_half(x, 1)
                elif x < Q_END:
                    if x % 4 == 3:
                        store_group(x)
                elif x % 2 == 1:
                    store_pair(x)
            if live(c):
                ev(c, 3)
                ev(c, 4)
            if c < G and live(c - 2):
                p2(c - 2)
            if live(c - 1):
                l1(c - 1, 0)
                l1(c - 1, 1)
            if c < G:
                qzh(c)
                qw(c)
            if live(c - 1):
                p1(c - 1, 0)
                p1(c - 1, 1)
            if live(c + 1):
                for k in range(3):
                    ta(c + 1, k)
